import numpy as np
import ml_dtypes


def mxq(x, axis, fmt="e4m3"):
    dtype, down = {"e4m3": (ml_dtypes.float8_e4m3fn, 7), "e5m2": (ml_dtypes.float8_e5m2, 14)}[fmt]
    v = np.moveaxis(np.asarray(x, np.float32).astype(ml_dtypes.bfloat16).astype(np.float64), axis, -1)
    blocks = v.reshape(v.shape[:-1] + (-1, 32))
    amax = np.abs(blocks).max(-1, keepdims=True)
    byte = np.maximum(np.where(amax > 0, np.frexp(amax)[1] - 1 + 127, 0) - down, 1)
    scale = np.exp2(byte - 127.0)
    codes = (blocks / scale).astype(np.float32).astype(dtype).astype(np.float64)
    return np.moveaxis((codes * scale).reshape(v.shape), -1, axis)


WIDE = False


def mx_kscale(k):
    if not WIDE:
        return np.ones(k)
    levels = np.array([10, -10, 5, -5, 0])
    a = np.random.permutation(np.resize(levels, k // 512 * 4)).reshape(k // 512, 4)
    idx = np.arange(k)
    return np.exp2(a[idx // 512, idx % 128 // 32])


BF16 = ml_dtypes.bfloat16


def bf(x):
    return np.asarray(x, np.float32).astype(BF16)


def f64(x):
    return np.asarray(x).astype(np.float64)


B, S, H, R = 2, 64, 4096, 1024
G = H // R


def setup_inputs():
    s = mx_kscale(R)
    return {"x": bf(np.random.standard_normal((B, S, H)) * np.tile(s, G)),
            "matrix": bf(np.random.standard_normal((R, R)) / np.sqrt(R) / s[:, None])}


def reference(x, matrix):
    x, matrix = f64(x), f64(matrix)
    b, n, h = x.shape
    r = matrix.shape[0]
    g = h // r
    compressed = x.reshape(b, n, g, r).sum(axis=2)
    out = mxq(compressed, 2, "e4m3") @ mxq(matrix, 0, "e4m3")
    return np.repeat(out, g, axis=2)[:, :, :h]

@@ -1,0 +1,122 @@
+from contextlib import ExitStack
+
+import concourse.mybir as mybir
+from concourse.masks import make_identity
+
+F32 = mybir.dt.float32
+BF16 = mybir.dt.bfloat16
+U32 = mybir.dt.uint32
+U8 = mybir.dt.uint8
+FP8X4 = mybir.dt.float8_e4m3fn_x4
+ADD = mybir.AluOpType.add
+
+P = 128
+PACK = 4
+K_PASS = P * PACK
+R = 1024
+GROUPS = 4
+PASSES = R // K_PASS
+CHUNK = 256
+CHUNKS = R // CHUNK
+BANK = 512
+VECTOR_COLS = 160
+RUN = 4
+
+FLOPS = 2 * P * R * R
+
+
+def tile_mora_s_kernel(tc, x, matrix, out):
+    nc = tc.nc
+    x_rows = x.flatten_outer_dims()
+    out_rows = out.flatten_outer_dims()
+    x_view = x_rows.rearrange("n (a b k) -> a n b k", a=GROUPS // 2, b=2)
+    m_view = matrix.rearrange("(s p) n -> p s n", p=P)
+
+    with ExitStack() as ctx:
+        const = ctx.enter_context(tc.tile_pool(name="const", bufs=1))
+        x_pool = ctx.enter_context(tc.tile_pool(name="x_pool", bufs=2))
+        m_pool = ctx.enter_context(tc.tile_pool(name="m_pool", bufs=CHUNKS))
+        t_psum = ctx.enter_context(tc.psum_pool(name="t_psum", bufs=PASSES))
+        y_psum = ctx.enter_context(tc.psum_pool(name="y_psum", bufs=CHUNKS))
+
+        ident = const.tile([P, P], F32)
+        make_identity(nc, ident[:])
+
+        x_pairs = []
+        for a in range(GROUPS // 2):
+            x_pair = x_pool.tile([P, 2, R], BF16, name="x_pair")
+            nc.sync.dma_start(out=x_pair[:], in_=x_view[a])
+            x_pairs.append(x_pair)
+        m_raw = []
+        for h in range(CHUNKS):
+            raw = m_pool.tile([P, PASSES * PACK, CHUNK], BF16, name="raw")
+            nc.sync.dma_start(out=raw[:], in_=m_view[:, :, h * CHUNK : (h + 1) * CHUNK])
+            m_raw.append(raw)
+
+        pair_sums = []
+        for a in range(GROUPS // 2):
+            pair_sum = x_pool.tile([P, R], F32, name="pair_sum")
+            nc.vector.tensor_tensor(
+                out=pair_sum[:], in0=x_pairs[a][:, 0, :], in1=x_pairs[a][:, 1, :], op=ADD
+            )
+            pair_sums.append(pair_sum)
+        c_f32 = const.tile([P, R], F32)
+        c_grouped = const.tile([P, PASSES, P, PACK], BF16, align_bytes=64)
+        for g in range(PASSES):
+            k_cols = slice(g * K_PASS, (g + 1) * K_PASS)
+            nc.vector.tensor_tensor(
+                out=c_f32[:, k_cols], in0=pair_sums[0][:, k_cols], in1=pair_sums[1][:, k_cols], op=ADD
+            )
+            c_t = t_psum.tile([P, PACK, P], F32, name="c_t")
+            for t in range(PACK):
+                first = g * K_PASS + t * P
+                nc.tensor.transpose(c_t[:, t, :], c_f32[:, first : first + P], ident[:])
+            nc.scalar.copy(out=c_grouped[:, g], in_=c_t[:].rearrange("p t n -> p n t"))
+        c_codes = const.tile([P, PASSES, P], U32, align_bytes=64)
+        c_scales = const.tile([P, PASSES, P], U8, align_bytes=64)
+        nc.vector.quantize_mx(
+            out=c_codes[:].rearrange("p g n -> p (g n)").bitcast(FP8X4),
+            scales=c_scales[:].rearrange("p g n -> p (g n)"),
+            in_=c_grouped[:].rearrange("p g n t -> p (g n t)"),
+        )
+
+        for h in range(CHUNKS):
+            raw = m_raw[h]
+            grouped = m_pool.tile([P, PASSES, CHUNK, PACK], BF16, name="grouped", align_bytes=64)
+            nc.vector.tensor_copy(
+                out=grouped[:, :, :VECTOR_COLS, :].rearrange("p g (c i) t -> p g c t i", i=RUN),
+                in_=raw[:, :, :VECTOR_COLS].rearrange("p (g t) (c i) -> p g c t i", t=PACK, i=RUN),
+            )
+            for g in range(PASSES):
+                nc.scalar.copy(
+                    out=grouped[:, g, VECTOR_COLS:, :].rearrange("p (c i) t -> p c t i", i=RUN),
+                    in_=raw[:, g * PACK : (g + 1) * PACK, VECTOR_COLS:].rearrange(
+                        "p t (c i) -> p c t i", i=RUN
+                    ),
+                )
+            codes = m_pool.tile([P, PASSES, CHUNK], U32, name="codes", align_bytes=64)
+            scales = m_pool.tile([P, PASSES, CHUNK], U8, name="scales", align_bytes=64)
+            nc.vector.quantize_mx(
+                out=codes[:].rearrange("p g c -> p (g c)").bitcast(FP8X4),
+                scales=scales[:].rearrange("p g c -> p (g c)"),
+                in_=grouped[:].rearrange("p g c t -> p (g c t)"),
+            )
+            y = y_psum.tile([P, BANK], F32, name="y")
+            for g in range(PASSES):
+                nc.tensor.matmul_mx(
+                    out=y[:, :CHUNK],
+                    lhsT=c_codes[:, g, :].bitcast(FP8X4),
+                    lhsT_scale=c_scales[:, g, :],
+                    rhs=codes[:, g, :].bitcast(FP8X4),
+                    rhs_scale=scales[:, g, :],
+                    start=(g == 0),
+                    stop=(g == PASSES - 1),
+                )
+            repeated = m_pool.tile([P, CHUNK, GROUPS], F32, name="repeated")
+            nc.scalar.copy(
+                out=repeated[:], in_=y[:, :CHUNK].unsqueeze(2).to_broadcast([P, CHUNK, GROUPS])
+            )
+            nc.sync.dma_start(
+                out=out_rows[:, h * CHUNK * GROUPS : (h + 1) * CHUNK * GROUPS],
+                in_=repeated[:].rearrange("p k j -> p (k j)"),
+            )

@@ -19,7 +19,7 @@ PASSES = R // K_PASS
 CHUNK = 256
 CHUNKS = R // CHUNK
 BANK = 512
-VECTOR_COLS = 160
+VECTOR_COLS = 192
 RUN = 4
 
 FLOPS = 2 * P * R * R
@@ -38,6 +38,7 @@ def tile_mora_s_kernel(tc, x, matrix, out):
         m_pool = ctx.enter_context(tc.tile_pool(name="m_pool", bufs=CHUNKS))
         t_psum = ctx.enter_context(tc.psum_pool(name="t_psum", bufs=PASSES))
         y_psum = ctx.enter_context(tc.psum_pool(name="y_psum", bufs=CHUNKS))
+        ctx.enter_context(tc.manual_schedule())
 
         ident = const.tile([P, P], F32)
         make_identity(nc, ident[:])
@@ -53,34 +54,47 @@ def tile_mora_s_kernel(tc, x, matrix, out):
             nc.sync.dma_start(out=raw[:], in_=m_view[:, :, h * CHUNK : (h + 1) * CHUNK])
             m_raw.append(raw)
 
-        pair_sums = []
+        c_t = []
+        for g in range(PASSES):
+            c_t.append(t_psum.tile([P, PACK, P], F32, name="c_t"))
         for a in range(GROUPS // 2):
             pair_sum = x_pool.tile([P, R], F32, name="pair_sum")
-            nc.vector.tensor_tensor(
-                out=pair_sum[:], in0=x_pairs[a][:, 0, :], in1=x_pairs[a][:, 1, :], op=ADD
-            )
-            pair_sums.append(pair_sum)
-        c_f32 = const.tile([P, R], F32)
+            for g in range(PASSES):
+                k_cols = slice(g * K_PASS, (g + 1) * K_PASS)
+                nc.vector.tensor_tensor(
+                    out=pair_sum[:, k_cols], in0=x_pairs[a][:, 0, k_cols], in1=x_pairs[a][:, 1, k_cols], op=ADD
+                )
+                for t in range(PACK):
+                    first = g * K_PASS + t * P
+                    nc.tensor.matmul(
+                        out=c_t[g][:, t, :],
+                        lhsT=pair_sum[:, first : first + P],
+                        rhs=ident[:],
+                        is_transpose=True,
+                        start=(a == 0 and t == 0),
+                        stop=(a == GROUPS // 2 - 1 and t == PACK - 1),
+                    )
+
         c_grouped = const.tile([P, PASSES, P, PACK], BF16, align_bytes=64)
-        for g in range(PASSES):
-            k_cols = slice(g * K_PASS, (g + 1) * K_PASS)
-            nc.vector.tensor_tensor(
-                out=c_f32[:, k_cols], in0=pair_sums[0][:, k_cols], in1=pair_sums[1][:, k_cols], op=ADD
-            )
-            c_t = t_psum.tile([P, PACK, P], F32, name="c_t")
-            for t in range(PACK):
-                first = g * K_PASS + t * P
-                nc.tensor.transpose(c_t[:, t, :], c_f32[:, first : first + P], ident[:])
-            nc.scalar.copy(out=c_grouped[:, g], in_=c_t[:].rearrange("p t n -> p n t"))
         c_codes = const.tile([P, PASSES, P], U32, align_bytes=64)
         c_scales = const.tile([P, PASSES, P], U8, align_bytes=64)
-        nc.vector.quantize_mx(
-            out=c_codes[:].rearrange("p g n -> p (g n)").bitcast(FP8X4),
-            scales=c_scales[:].rearrange("p g n -> p (g n)"),
-            in_=c_grouped[:].rearrange("p g n t -> p (g n t)"),
-        )
 
-        for h in range(CHUNKS):
+        def round_c():
+            for g in range(PASSES):
+                nc.scalar.copy(out=c_grouped[:, g], in_=c_t[g][:].rearrange("p t n -> p n t"))
+
+        def quantise_c():
+            nc.vector.quantize_mx(
+                out=c_codes[:].rearrange("p g n -> p (g n)").bitcast(FP8X4),
+                scales=c_scales[:].rearrange("p g n -> p (g n)"),
+                in_=c_grouped[:].rearrange("p g n t -> p (g n t)"),
+            )
+
+        m_grouped = []
+        m_codes = []
+        m_scales = []
+
+        def regroup(h):
             raw = m_raw[h]
             grouped = m_pool.tile([P, PASSES, CHUNK, PACK], BF16, name="grouped", align_bytes=64)
             nc.vector.tensor_copy(
@@ -94,29 +108,47 @@ def tile_mora_s_kernel(tc, x, matrix, out):
                         "p t (c i) -> p c t i", i=RUN
                     ),
                 )
+            m_grouped.append(grouped)
+
+        def quantise(h):
             codes = m_pool.tile([P, PASSES, CHUNK], U32, name="codes", align_bytes=64)
             scales = m_pool.tile([P, PASSES, CHUNK], U8, name="scales", align_bytes=64)
             nc.vector.quantize_mx(
                 out=codes[:].rearrange("p g c -> p (g c)").bitcast(FP8X4),
                 scales=scales[:].rearrange("p g c -> p (g c)"),
-                in_=grouped[:].rearrange("p g c t -> p (g c t)"),
+                in_=m_grouped[h][:].rearrange("p g c t -> p (g c t)"),
             )
+            m_codes.append(codes)
+            m_scales.append(scales)
+
+        def multiply_and_store(h):
             y = y_psum.tile([P, BANK], F32, name="y")
             for g in range(PASSES):
                 nc.tensor.matmul_mx(
                     out=y[:, :CHUNK],
                     lhsT=c_codes[:, g, :].bitcast(FP8X4),
                     lhsT_scale=c_scales[:, g, :],
-                    rhs=codes[:, g, :].bitcast(FP8X4),
-                    rhs_scale=scales[:, g, :],
+                    rhs=m_codes[h][:, g, :].bitcast(FP8X4),
+                    rhs_scale=m_scales[h][:, g, :],
                     start=(g == 0),
                     stop=(g == PASSES - 1),
                 )
             repeated = m_pool.tile([P, CHUNK, GROUPS], F32, name="repeated")
-            nc.scalar.copy(
-                out=repeated[:], in_=y[:, :CHUNK].unsqueeze(2).to_broadcast([P, CHUNK, GROUPS])
-            )
+            copy_out = nc.vector.tensor_copy if h == CHUNKS - 1 else nc.scalar.copy
+            copy_out(out=repeated[:], in_=y[:, :CHUNK].unsqueeze(2).to_broadcast([P, CHUNK, GROUPS]))
             nc.sync.dma_start(
                 out=out_rows[:, h * CHUNK * GROUPS : (h + 1) * CHUNK * GROUPS],
                 in_=repeated[:].rearrange("p k j -> p (k j)"),
             )
+
+        for h in range(CHUNKS + 2):
+            if h < CHUNKS:
+                regroup(h)
+            if h == 0:
+                round_c()
+            if h == 1:
+                quantise_c()
+            if 1 <= h <= CHUNKS:
+                quantise(h - 1)
+            if h >= 2:
+                multiply_and_store(h - 2)

@@ -37,7 +37,7 @@ def tile_mora_s_kernel(tc, x, matrix, out):
         x_pool = ctx.enter_context(tc.tile_pool(name="x_pool", bufs=2))
         m_pool = ctx.enter_context(tc.tile_pool(name="m_pool", bufs=CHUNKS))
         t_psum = ctx.enter_context(tc.psum_pool(name="t_psum", bufs=PASSES))
-        y_psum = ctx.enter_context(tc.psum_pool(name="y_psum", bufs=CHUNKS))
+        y_psum = ctx.enter_context(tc.psum_pool(name="y_psum", bufs=CHUNKS + 1))
         ctx.enter_context(tc.manual_schedule())
 
         ident = const.tile([P, P], F32)
@@ -122,24 +122,34 @@ def tile_mora_s_kernel(tc, x, matrix, out):
             m_scales.append(scales)
 
         def multiply_and_store(h):
-            y = y_psum.tile([P, BANK], F32, name="y")
-            for g in range(PASSES):
-                nc.tensor.matmul_mx(
-                    out=y[:, :CHUNK],
-                    lhsT=c_codes[:, g, :].bitcast(FP8X4),
-                    lhsT_scale=c_scales[:, g, :],
-                    rhs=m_codes[h][:, g, :].bitcast(FP8X4),
-                    rhs_scale=m_scales[h][:, g, :],
-                    start=(g == 0),
-                    stop=(g == PASSES - 1),
-                )
+            if h == CHUNKS - 1:
+                copies_out = (nc.vector.tensor_copy, nc.scalar.copy)
+            else:
+                copies_out = (nc.scalar.copy,)
+            width = CHUNK // len(copies_out)
             repeated = m_pool.tile([P, CHUNK, GROUPS], F32, name="repeated")
-            copy_out = nc.vector.tensor_copy if h == CHUNKS - 1 else nc.scalar.copy
-            copy_out(out=repeated[:], in_=y[:, :CHUNK].unsqueeze(2).to_broadcast([P, CHUNK, GROUPS]))
-            nc.sync.dma_start(
-                out=out_rows[:, h * CHUNK * GROUPS : (h + 1) * CHUNK * GROUPS],
-                in_=repeated[:].rearrange("p k j -> p (k j)"),
-            )
+            for e, copy_out in enumerate(copies_out):
+                cols = slice(e * width, (e + 1) * width)
+                y = y_psum.tile([P, BANK], F32, name="y")
+                for g in range(PASSES):
+                    nc.tensor.matmul_mx(
+                        out=y[:, :width],
+                        lhsT=c_codes[:, g, :].bitcast(FP8X4),
+                        lhsT_scale=c_scales[:, g, :],
+                        rhs=m_codes[h][:, g, cols].bitcast(FP8X4),
+                        rhs_scale=m_scales[h][:, g, cols],
+                        start=(g == 0),
+                        stop=(g == PASSES - 1),
+                    )
+                copy_out(
+                    out=repeated[:, cols, :],
+                    in_=y[:, :width].unsqueeze(2).to_broadcast([P, width, GROUPS]),
+                )
+                first = (h * CHUNK + e * width) * GROUPS
+                nc.sync.dma_start(
+                    out=out_rows[:, first : first + width * GROUPS],
+                    in_=repeated[:, cols, :].rearrange("p k j -> p (k j)"),
+                )
 
         for h in range(CHUNKS + 2):
             if h < CHUNKS:
@@ -148,7 +158,7 @@ def tile_mora_s_kernel(tc, x, matrix, out):
                 round_c()
             if h == 1:
                 quantise_c()
-            if 1 <= h <= CHUNKS:
-                quantise(h - 1)
+            if h < CHUNKS:
+                quantise(h)
             if h >= 2:
                 multiply_and_store(h - 2)

@@ -16,11 +16,14 @@ K_PASS = P * PACK
 R = 1024
 GROUPS = 4
 PASSES = R // K_PASS
-CHUNK = 256
-CHUNKS = R // CHUNK
+HALF = 512
+HALVES = R // HALF
+PART = 256
+PARTS = HALF // PART
 BANK = 512
-VECTOR_COLS = 192
+VECTOR_COLS = 352
 RUN = 4
+LAST = 128
 
 FLOPS = 2 * P * R * R
 
@@ -35,9 +38,10 @@ def tile_mora_s_kernel(tc, x, matrix, out):
     with ExitStack() as ctx:
         const = ctx.enter_context(tc.tile_pool(name="const", bufs=1))
         x_pool = ctx.enter_context(tc.tile_pool(name="x_pool", bufs=2))
-        m_pool = ctx.enter_context(tc.tile_pool(name="m_pool", bufs=CHUNKS))
+        m_pool = ctx.enter_context(tc.tile_pool(name="m_pool", bufs=HALVES * PASSES))
+        o_pool = ctx.enter_context(tc.tile_pool(name="o_pool", bufs=6))
         t_psum = ctx.enter_context(tc.psum_pool(name="t_psum", bufs=PASSES))
-        y_psum = ctx.enter_context(tc.psum_pool(name="y_psum", bufs=CHUNKS + 1))
+        y_psum = ctx.enter_context(tc.psum_pool(name="y_psum", bufs=6))
         ctx.enter_context(tc.manual_schedule())
 
         ident = const.tile([P, P], F32)
@@ -49,9 +53,12 @@ def tile_mora_s_kernel(tc, x, matrix, out):
             nc.sync.dma_start(out=x_pair[:], in_=x_view[a])
             x_pairs.append(x_pair)
         m_raw = []
-        for h in range(CHUNKS):
-            raw = m_pool.tile([P, PASSES * PACK, CHUNK], BF16, name="raw")
-            nc.sync.dma_start(out=raw[:], in_=m_view[:, :, h * CHUNK : (h + 1) * CHUNK])
+        for u in range(HALVES * PASSES):
+            h, g = divmod(u, PASSES)
+            raw = m_pool.tile([P, PACK, HALF], BF16, name="raw")
+            nc.sync.dma_start(
+                out=raw[:], in_=m_view[:, g * PACK : (g + 1) * PACK, h * HALF : (h + 1) * HALF]
+            )
             m_raw.append(raw)
 
         c_t = []
@@ -94,71 +101,84 @@ def tile_mora_s_kernel(tc, x, matrix, out):
         m_codes = []
         m_scales = []
 
-        def regroup(h):
-            raw = m_raw[h]
-            grouped = m_pool.tile([P, PASSES, CHUNK, PACK], BF16, name="grouped", align_bytes=64)
-            nc.vector.tensor_copy(
-                out=grouped[:, :, :VECTOR_COLS, :].rearrange("p g (c i) t -> p g c t i", i=RUN),
-                in_=raw[:, :, :VECTOR_COLS].rearrange("p (g t) (c i) -> p g c t i", t=PACK, i=RUN),
-            )
-            for g in range(PASSES):
-                nc.scalar.copy(
-                    out=grouped[:, g, VECTOR_COLS:, :].rearrange("p (c i) t -> p c t i", i=RUN),
-                    in_=raw[:, g * PACK : (g + 1) * PACK, VECTOR_COLS:].rearrange(
-                        "p t (c i) -> p c t i", i=RUN
-                    ),
+        def regroup(u):
+            raw = m_raw[u]
+            grouped = m_pool.tile([P, HALF, PACK], BF16, name="grouped", align_bytes=64)
+            for copy, cols in (
+                (nc.vector.tensor_copy, slice(0, VECTOR_COLS)),
+                (nc.scalar.copy, slice(VECTOR_COLS, HALF)),
+            ):
+                copy(
+                    out=grouped[:, cols, :].rearrange("p (c i) t -> p c t i", i=RUN),
+                    in_=raw[:, :, cols].rearrange("p t (c i) -> p c t i", i=RUN),
                 )
             m_grouped.append(grouped)
+            m_codes.append(m_pool.tile([P, HALF], U32, name="codes", align_bytes=64))
+            m_scales.append(m_pool.tile([P, HALF], U8, name="scales", align_bytes=64))
 
-        def quantise(h):
-            codes = m_pool.tile([P, PASSES, CHUNK], U32, name="codes", align_bytes=64)
-            scales = m_pool.tile([P, PASSES, CHUNK], U8, name="scales", align_bytes=64)
+        def quantise(u, q):
+            cols = slice(q * PART, (q + 1) * PART)
             nc.vector.quantize_mx(
-                out=codes[:].rearrange("p g c -> p (g c)").bitcast(FP8X4),
-                scales=scales[:].rearrange("p g c -> p (g c)"),
-                in_=m_grouped[h][:].rearrange("p g c t -> p (g c t)"),
+                out=m_codes[u][:, cols].bitcast(FP8X4),
+                scales=m_scales[u][:, cols],
+                in_=m_grouped[u][:, cols, :].rearrange("p c t -> p (c t)"),
             )
-            m_codes.append(codes)
-            m_scales.append(scales)
 
-        def multiply_and_store(h):
-            if h == CHUNKS - 1:
-                copies_out = (nc.vector.tensor_copy, nc.scalar.copy)
-            else:
-                copies_out = (nc.scalar.copy,)
-            width = CHUNK // len(copies_out)
-            repeated = m_pool.tile([P, CHUNK, GROUPS], F32, name="repeated")
-            for e, copy_out in enumerate(copies_out):
-                cols = slice(e * width, (e + 1) * width)
-                y = y_psum.tile([P, BANK], F32, name="y")
-                for g in range(PASSES):
-                    nc.tensor.matmul_mx(
-                        out=y[:, :width],
-                        lhsT=c_codes[:, g, :].bitcast(FP8X4),
-                        lhsT_scale=c_scales[:, g, :],
-                        rhs=m_codes[h][:, g, cols].bitcast(FP8X4),
-                        rhs_scale=m_scales[h][:, g, cols],
-                        start=(g == 0),
-                        stop=(g == PASSES - 1),
-                    )
-                copy_out(
-                    out=repeated[:, cols, :],
-                    in_=y[:, :width].unsqueeze(2).to_broadcast([P, width, GROUPS]),
-                )
-                first = (h * CHUNK + e * width) * GROUPS
-                nc.sync.dma_start(
-                    out=out_rows[:, first : first + width * GROUPS],
-                    in_=repeated[:, cols, :].rearrange("p k j -> p (k j)"),
-                )
+        banks = {}
 
-        for h in range(CHUNKS + 2):
-            if h < CHUNKS:
-                regroup(h)
-            if h == 0:
-                round_c()
-            if h == 1:
-                quantise_c()
-            if h < CHUNKS:
-                quantise(h)
-            if h >= 2:
-                multiply_and_store(h - 2)
+        def multiply(h, g, first, width):
+            if g == 0:
+                banks[(h, first)] = y_psum.tile([P, BANK], F32, name="y")
+            u = h * PASSES + g
+            nc.tensor.matmul_mx(
+                out=banks[(h, first)][:, :width],
+                lhsT=c_codes[:, g, :].bitcast(FP8X4),
+                lhsT_scale=c_scales[:, g, :],
+                rhs=m_codes[u][:, first : first + width].bitcast(FP8X4),
+                rhs_scale=m_scales[u][:, first : first + width],
+                start=(g == 0),
+                stop=(g == PASSES - 1),
+            )
+
+        def repeat_and_store(copy_out, h, first, width):
+            repeated = o_pool.tile([P, PART, GROUPS], F32, name="repeated")
+            copy_out(
+                out=repeated[:, :width, :],
+                in_=banks[(h, first)][:, :width].unsqueeze(2).to_broadcast([P, width, GROUPS]),
+            )
+            start = (h * HALF + first) * GROUPS
+            nc.sync.dma_start(
+                out=out_rows[:, start : start + width * GROUPS],
+                in_=repeated[:, :width, :].rearrange("p k j -> p (k j)"),
+            )
+
+        regroup(0)
+        round_c()
+        quantise(0, 0)
+        regroup(1)
+        quantise(0, 1)
+        quantise_c()
+        multiply(0, 0, 0, PART)
+        multiply(0, 0, PART, PART)
+        quantise(1, 0)
+        multiply(0, 1, 0, PART)
+        regroup(2)
+        repeat_and_store(nc.scalar.copy, 0, 0, PART)
+        quantise(1, 1)
+        multiply(0, 1, PART, PART)
+        quantise(2, 0)
+        regroup(3)
+        repeat_and_store(nc.scalar.copy, 0, PART, PART)
+        quantise(2, 1)
+        for e in range(HALF // LAST):
+            multiply(1, 0, e * LAST, LAST)
+        quantise(3, 0)
+        multiply(1, 1, 0, LAST)
+        multiply(1, 1, LAST, LAST)
+        repeat_and_store(nc.scalar.copy, 1, 0, LAST)
+        repeat_and_store(nc.scalar.copy, 1, LAST, LAST)
+        quantise(3, 1)
+        multiply(1, 1, 2 * LAST, LAST)
+        multiply(1, 1, 3 * LAST, LAST)
+        repeat_and_store(nc.vector.tensor_copy, 1, 2 * LAST, LAST)
+        repeat_and_store(nc.vector.tensor_copy, 1, 3 * LAST, LAST)

@@ -22,6 +22,7 @@ PART = 256
 PARTS = HALF // PART
 BANK = 512
 VECTOR_COLS = 352
+LAST_VECTOR_COLS = 416
 RUN = 4
 LAST = 128
 
@@ -56,9 +57,14 @@ def tile_mora_s_kernel(tc, x, matrix, out):
         for u in range(HALVES * PASSES):
             h, g = divmod(u, PASSES)
             raw = m_pool.tile([P, PACK, HALF], BF16, name="raw")
-            nc.sync.dma_start(
-                out=raw[:], in_=m_view[:, g * PACK : (g + 1) * PACK, h * HALF : (h + 1) * HALF]
-            )
+            pieces = PARTS if u == HALVES * PASSES - 1 else 1
+            width = HALF // pieces
+            for q in range(pieces):
+                first = h * HALF + q * width
+                nc.sync.dma_start(
+                    out=raw[:, :, q * width : (q + 1) * width],
+                    in_=m_view[:, g * PACK : (g + 1) * PACK, first : first + width],
+                )
             m_raw.append(raw)
 
         c_t = []
@@ -101,20 +107,21 @@ def tile_mora_s_kernel(tc, x, matrix, out):
         m_codes = []
         m_scales = []
 
-        def regroup(u):
-            raw = m_raw[u]
-            grouped = m_pool.tile([P, HALF, PACK], BF16, name="grouped", align_bytes=64)
-            for copy, cols in (
-                (nc.vector.tensor_copy, slice(0, VECTOR_COLS)),
-                (nc.scalar.copy, slice(VECTOR_COLS, HALF)),
-            ):
-                copy(
-                    out=grouped[:, cols, :].rearrange("p (c i) t -> p c t i", i=RUN),
-                    in_=raw[:, :, cols].rearrange("p t (c i) -> p c t i", i=RUN),
-                )
-            m_grouped.append(grouped)
+        def new_tiles():
+            m_grouped.append(m_pool.tile([P, HALF, PACK], BF16, name="grouped", align_bytes=64))
             m_codes.append(m_pool.tile([P, HALF], U32, name="codes", align_bytes=64))
             m_scales.append(m_pool.tile([P, HALF], U8, name="scales", align_bytes=64))
+
+        def regroup_cols(copy, u, first, last):
+            copy(
+                out=m_grouped[u][:, first:last, :].rearrange("p (c i) t -> p c t i", i=RUN),
+                in_=m_raw[u][:, :, first:last].rearrange("p t (c i) -> p c t i", i=RUN),
+            )
+
+        def regroup(u):
+            new_tiles()
+            regroup_cols(nc.vector.tensor_copy, u, 0, VECTOR_COLS)
+            regroup_cols(nc.scalar.copy, u, VECTOR_COLS, HALF)
 
         def quantise(u, q):
             cols = slice(q * PART, (q + 1) * PART)
@@ -167,11 +174,14 @@ def tile_mora_s_kernel(tc, x, matrix, out):
         quantise(1, 1)
         multiply(0, 1, PART, PART)
         quantise(2, 0)
-        regroup(3)
+        new_tiles()
+        regroup_cols(nc.vector.tensor_copy, 3, 0, PART)
         repeat_and_store(nc.scalar.copy, 0, PART, PART)
         quantise(2, 1)
         for e in range(HALF // LAST):
             multiply(1, 0, e * LAST, LAST)
+        regroup_cols(nc.vector.tensor_copy, 3, PART, LAST_VECTOR_COLS)
+        regroup_cols(nc.scalar.copy, 3, LAST_VECTOR_COLS, HALF)
         quantise(3, 0)
         multiply(1, 1, 0, LAST)
         multiply(1, 1, LAST, LAST)

@@ -22,7 +22,6 @@ PART = 256
 PARTS = HALF // PART
 BANK = 512
 VECTOR_COLS = 352
-LAST_VECTOR_COLS = 416
 RUN = 4
 LAST = 128
 
@@ -40,9 +39,8 @@ def tile_mora_s_kernel(tc, x, matrix, out):
         const = ctx.enter_context(tc.tile_pool(name="const", bufs=1))
         x_pool = ctx.enter_context(tc.tile_pool(name="x_pool", bufs=2))
         m_pool = ctx.enter_context(tc.tile_pool(name="m_pool", bufs=HALVES * PASSES))
-        o_pool = ctx.enter_context(tc.tile_pool(name="o_pool", bufs=6))
-        t_psum = ctx.enter_context(tc.psum_pool(name="t_psum", bufs=PASSES))
-        y_psum = ctx.enter_context(tc.psum_pool(name="y_psum", bufs=6))
+        o_pool = ctx.enter_context(tc.tile_pool(name="o_pool", bufs=7))
+        psum = ctx.enter_context(tc.psum_pool(name="psum", bufs=8))
         ctx.enter_context(tc.manual_schedule())
 
         ident = const.tile([P, P], F32)
@@ -69,7 +67,7 @@ def tile_mora_s_kernel(tc, x, matrix, out):
 
         c_t = []
         for g in range(PASSES):
-            c_t.append(t_psum.tile([P, PACK, P], F32, name="c_t"))
+            c_t.append(psum.tile([P, PACK, P], F32, name="bank"))
         for a in range(GROUPS // 2):
             pair_sum = x_pool.tile([P, R], F32, name="pair_sum")
             for g in range(PASSES):
@@ -135,7 +133,7 @@ def tile_mora_s_kernel(tc, x, matrix, out):
 
         def multiply(h, g, first, width):
             if g == 0:
-                banks[(h, first)] = y_psum.tile([P, BANK], F32, name="y")
+                banks[(h, first)] = psum.tile([P, BANK], F32, name="bank")
             u = h * PASSES + g
             nc.tensor.matmul_mx(
                 out=banks[(h, first)][:, :width],
@@ -165,30 +163,34 @@ def tile_mora_s_kernel(tc, x, matrix, out):
         regroup(1)
         quantise(0, 1)
         quantise_c()
-        multiply(0, 0, 0, PART)
+        multiply(0, 0, 0, LAST)
+        multiply(0, 0, LAST, LAST)
         multiply(0, 0, PART, PART)
         quantise(1, 0)
-        multiply(0, 1, 0, PART)
+        multiply(0, 1, 0, LAST)
+        multiply(0, 1, LAST, LAST)
         regroup(2)
-        repeat_and_store(nc.scalar.copy, 0, 0, PART)
+        repeat_and_store(nc.scalar.copy, 0, 0, LAST)
+        repeat_and_store(nc.scalar.copy, 0, LAST, LAST)
         quantise(1, 1)
         multiply(0, 1, PART, PART)
-        quantise(2, 0)
         new_tiles()
         regroup_cols(nc.vector.tensor_copy, 3, 0, PART)
         repeat_and_store(nc.scalar.copy, 0, PART, PART)
-        quantise(2, 1)
-        for e in range(HALF // LAST):
-            multiply(1, 0, e * LAST, LAST)
-        regroup_cols(nc.vector.tensor_copy, 3, PART, LAST_VECTOR_COLS)
-        regroup_cols(nc.scalar.copy, 3, LAST_VECTOR_COLS, HALF)
+        quantise(2, 0)
+        multiply(1, 0, 0, LAST)
+        multiply(1, 0, LAST, LAST)
         quantise(3, 0)
         multiply(1, 1, 0, LAST)
         multiply(1, 1, LAST, LAST)
         repeat_and_store(nc.scalar.copy, 1, 0, LAST)
-        repeat_and_store(nc.scalar.copy, 1, LAST, LAST)
+        regroup_cols(nc.vector.tensor_copy, 3, PART, HALF)
+        quantise(2, 1)
+        multiply(1, 0, 2 * LAST, LAST)
+        multiply(1, 0, 3 * LAST, LAST)
         quantise(3, 1)
         multiply(1, 1, 2 * LAST, LAST)
         multiply(1, 1, 3 * LAST, LAST)
-        repeat_and_store(nc.vector.tensor_copy, 1, 2 * LAST, LAST)
+        repeat_and_store(nc.vector.tensor_copy, 1, LAST, LAST)
+        repeat_and_store(nc.scalar.copy, 1, 2 * LAST, LAST)
         repeat_and_store(nc.vector.tensor_copy, 1, 3 * LAST, LAST)

from contextlib import ExitStack

import concourse.mybir as mybir
from concourse.masks import make_identity

F32 = mybir.dt.float32
BF16 = mybir.dt.bfloat16
U32 = mybir.dt.uint32
U8 = mybir.dt.uint8
FP8X4 = mybir.dt.float8_e4m3fn_x4
ADD = mybir.AluOpType.add

P = 128
PACK = 4
K_PASS = P * PACK
R = 1024
GROUPS = 4
PASSES = R // K_PASS
HALF = 512
HALVES = R // HALF
PART = 256
PARTS = HALF // PART
BANK = 512
VECTOR_COLS = 352
RUN = 4
LAST = 128

FLOPS = 2 * P * R * R


def tile_mora_s_kernel(tc, x, matrix, out):
    nc = tc.nc
    x_rows = x.flatten_outer_dims()
    out_rows = out.flatten_outer_dims()
    x_view = x_rows.rearrange("n (a b k) -> a n b k", a=GROUPS // 2, b=2)
    m_view = matrix.rearrange("(s p) n -> p s n", p=P)

    with ExitStack() as ctx:
        const = ctx.enter_context(tc.tile_pool(name="const", bufs=1))
        x_pool = ctx.enter_context(tc.tile_pool(name="x_pool", bufs=2))
        m_pool = ctx.enter_context(tc.tile_pool(name="m_pool", bufs=HALVES * PASSES))
        o_pool = ctx.enter_context(tc.tile_pool(name="o_pool", bufs=7))
        psum = ctx.enter_context(tc.psum_pool(name="psum", bufs=8))
        ctx.enter_context(tc.manual_schedule())

        ident = const.tile([P, P], F32)
        make_identity(nc, ident[:])

        x_pairs = []
        for a in range(GROUPS // 2):
            x_pair = x_pool.tile([P, 2, R], BF16, name="x_pair")
            nc.sync.dma_start(out=x_pair[:], in_=x_view[a])
            x_pairs.append(x_pair)
        m_raw = []
        for u in range(HALVES * PASSES):
            h, g = divmod(u, PASSES)
            raw = m_pool.tile([P, PACK, HALF], BF16, name="raw")
            pieces = PARTS if u == HALVES * PASSES - 1 else 1
            width = HALF // pieces
            for q in range(pieces):
                first = h * HALF + q * width
                nc.sync.dma_start(
                    out=raw[:, :, q * width : (q + 1) * width],
                    in_=m_view[:, g * PACK : (g + 1) * PACK, first : first + width],
                )
            m_raw.append(raw)

        c_t = []
        for g in range(PASSES):
            c_t.append(psum.tile([P, PACK, P], F32, name="bank"))
        for a in range(GROUPS // 2):
            pair_sum = x_pool.tile([P, R], F32, name="pair_sum")
            for g in range(PASSES):
                k_cols = slice(g * K_PASS, (g + 1) * K_PASS)
                nc.vector.tensor_tensor(
                    out=pair_sum[:, k_cols], in0=x_pairs[a][:, 0, k_cols], in1=x_pairs[a][:, 1, k_cols], op=ADD
                )
                for t in range(PACK):
                    first = g * K_PASS + t * P
                    nc.tensor.matmul(
                        out=c_t[g][:, t, :],
                        lhsT=pair_sum[:, first : first + P],
                        rhs=ident[:],
                        is_transpose=True,
                        start=(a == 0 and t == 0),
                        stop=(a == GROUPS // 2 - 1 and t == PACK - 1),
                    )

        c_grouped = const.tile([P, PASSES, P, PACK], BF16, align_bytes=64)
        c_codes = const.tile([P, PASSES, P], U32, align_bytes=64)
        c_scales = const.tile([P, PASSES, P], U8, align_bytes=64)

        def round_c():
            for g in range(PASSES):
                nc.scalar.copy(out=c_grouped[:, g], in_=c_t[g][:].rearrange("p t n -> p n t"))

        def quantise_c():
            nc.vector.quantize_mx(
                out=c_codes[:].rearrange("p g n -> p (g n)").bitcast(FP8X4),
                scales=c_scales[:].rearrange("p g n -> p (g n)"),
                in_=c_grouped[:].rearrange("p g n t -> p (g n t)"),
            )

        m_grouped = []
        m_codes = []
        m_scales = []

        def new_tiles():
            m_grouped.append(m_pool.tile([P, HALF, PACK], BF16, name="grouped", align_bytes=64))
            m_codes.append(m_pool.tile([P, HALF], U32, name="codes", align_bytes=64))
            m_scales.append(m_pool.tile([P, HALF], U8, name="scales", align_bytes=64))

        def regroup_cols(copy, u, first, last):
            copy(
                out=m_grouped[u][:, first:last, :].rearrange("p (c i) t -> p c t i", i=RUN),
                in_=m_raw[u][:, :, first:last].rearrange("p t (c i) -> p c t i", i=RUN),
            )

        def regroup(u):
            new_tiles()
            regroup_cols(nc.vector.tensor_copy, u, 0, VECTOR_COLS)
            regroup_cols(nc.scalar.copy, u, VECTOR_COLS, HALF)

        def quantise(u, q):
            cols = slice(q * PART, (q + 1) * PART)
            nc.vector.quantize_mx(
                out=m_codes[u][:, cols].bitcast(FP8X4),
                scales=m_scales[u][:, cols],
                in_=m_grouped[u][:, cols, :].rearrange("p c t -> p (c t)"),
            )

        banks = {}

        def multiply(h, g, first, width):
            if g == 0:
                banks[(h, first)] = psum.tile([P, BANK], F32, name="bank")
            u = h * PASSES + g
            nc.tensor.matmul_mx(
                out=banks[(h, first)][:, :width],
                lhsT=c_codes[:, g, :].bitcast(FP8X4),
                lhsT_scale=c_scales[:, g, :],
                rhs=m_codes[u][:, first : first + width].bitcast(FP8X4),
                rhs_scale=m_scales[u][:, first : first + width],
                start=(g == 0),
                stop=(g == PASSES - 1),
            )

        def repeat_and_store(copy_out, h, first, width):
            repeated = o_pool.tile([P, PART, GROUPS], F32, name="repeated")
            copy_out(
                out=repeated[:, :width, :],
                in_=banks[(h, first)][:, :width].unsqueeze(2).to_broadcast([P, width, GROUPS]),
            )
            start = (h * HALF + first) * GROUPS
            nc.sync.dma_start(
                out=out_rows[:, start : start + width * GROUPS],
                in_=repeated[:, :width, :].rearrange("p k j -> p (k j)"),
            )

        regroup(0)
        round_c()
        quantise(0, 0)
        regroup(1)
        quantise(0, 1)
        quantise_c()
        multiply(0, 0, 0, LAST)
        multiply(0, 0, LAST, LAST)
        multiply(0, 0, PART, PART)
        quantise(1, 0)
        multiply(0, 1, 0, LAST)
        multiply(0, 1, LAST, LAST)
        regroup(2)
        repeat_and_store(nc.scalar.copy, 0, 0, LAST)
        repeat_and_store(nc.scalar.copy, 0, LAST, LAST)
        quantise(1, 1)
        multiply(0, 1, PART, PART)
        new_tiles()
        regroup_cols(nc.vector.tensor_copy, 3, 0, PART)
        repeat_and_store(nc.scalar.copy, 0, PART, PART)
        quantise(2, 0)
        multiply(1, 0, 0, LAST)
        multiply(1, 0, LAST, LAST)
        quantise(3, 0)
        multiply(1, 1, 0, LAST)
        multiply(1, 1, LAST, LAST)
        repeat_and_store(nc.scalar.copy, 1, 0, LAST)
        regroup_cols(nc.vector.tensor_copy, 3, PART, HALF)
        quantise(2, 1)
        multiply(1, 0, 2 * LAST, LAST)
        multiply(1, 0, 3 * LAST, LAST)
        quantise(3, 1)
        multiply(1, 1, 2 * LAST, LAST)
        multiply(1, 1, 3 * LAST, LAST)
        repeat_and_store(nc.vector.tensor_copy, 1, LAST, LAST)
        repeat_and_store(nc.scalar.copy, 1, 2 * LAST, LAST)
        repeat_and_store(nc.vector.tensor_copy, 1, 3 * LAST, LAST)
